import numpy as np
import ml_dtypes


def mxq(x, axis, fmt="e4m3"):
    dtype, down = {"e4m3": (ml_dtypes.float8_e4m3fn, 7), "e5m2": (ml_dtypes.float8_e5m2, 14)}[fmt]
    v = np.moveaxis(np.asarray(x, np.float32).astype(ml_dtypes.bfloat16).astype(np.float64), axis, -1)
    blocks = v.reshape(v.shape[:-1] + (-1, 32))
    amax = np.abs(blocks).max(-1, keepdims=True)
    byte = np.maximum(np.where(amax > 0, np.frexp(amax)[1] - 1 + 127, 0) - down, 1)
    scale = np.exp2(byte - 127.0)
    codes = (blocks / scale).astype(np.float32).astype(dtype).astype(np.float64)
    return np.moveaxis((codes * scale).reshape(v.shape), -1, axis)


WIDE = False


def mx_kscale(k):
    if not WIDE:
        return np.ones(k)
    levels = np.array([10, -10, 5, -5, 0])
    a = np.random.permutation(np.resize(levels, k // 512 * 4)).reshape(k // 512, 4)
    idx = np.arange(k)
    return np.exp2(a[idx // 512, idx % 128 // 32])


BF16 = ml_dtypes.bfloat16


def bf(x):
    return np.asarray(x, np.float32).astype(BF16)


def f64(x):
    return np.asarray(x).astype(np.float64)


E2M1 = np.array([0.0, 0.5, 1.0, 1.5, 2.0, 3.0, 4.0, 6.0, -0.0, -0.5, -1.0, -1.5, -2.0, -3.0, -4.0, -6.0])


def pack_weight(w, fmt):
    k, n = w.shape
    w = f64(bf(w)).reshape(k // 32, 32, n)
    amax = np.abs(w).max(1)
    if fmt == "e4m3":
        byte = np.frexp(amax)[1] - 1 + 127 - 7
    else:
        mant, ex = np.frexp(amax / 6.0)
        byte = np.where(mant > 0.5, ex, ex - 1) + 127
    byte = np.clip(np.where(amax > 0, byte, 1), 1, 254)
    scaled = (w * np.exp2(127.0 - byte)[:, None, :]).reshape(k, n).astype(np.float32)
    by_word = np.ascontiguousarray(scaled.reshape(k // 512, 128, 4, n).transpose(0, 1, 3, 2))
    if fmt == "e4m3":
        words = by_word.astype(ml_dtypes.float8_e4m3fn).view(np.uint8)
    else:
        c = by_word.astype(ml_dtypes.float4_e2m1fn).view(np.uint8) & 0xF
        words = c[..., 0::2] | (c[..., 1::2] << 4)
    return np.ascontiguousarray(words), np.ascontiguousarray(byte.astype(np.uint8).reshape(k // 512, 16, n))


def unpack_weight(words, scales, fmt):
    g, p, n, _ = words.shape
    if fmt == "e4m3":
        vals = np.ascontiguousarray(words).view(ml_dtypes.float8_e4m3fn).astype(np.float64)
    else:
        nib = np.empty((g, p, n, 4), np.uint8)
        nib[..., 0::2] = words & 0xF
        nib[..., 1::2] = words >> 4
        vals = E2M1[nib]
    vals = vals * np.repeat(np.exp2(scales.astype(np.float64) - 127.0), 8, axis=1)[..., None]
    return vals.transpose(0, 1, 3, 2).reshape(g * 512, n)

def pack4(w):
    words, scales = pack_weight(w, "e2m1")
    return words.reshape(words.shape[0], 128, -1), scales


def unpack4(words, scales):
    return unpack_weight(words.reshape(words.shape[0], 128, -1, 2), scales, "e2m1")


B, H, L, DM, DK, DV = 2, 4, 1024, 512, 128, 1024


def rotate_every_two(x):
    x1 = x[..., ::2]
    x2 = x[..., 1::2]
    return np.stack((-x2, x1), axis=-1).reshape(x.shape)


def xpos_sincos(length, dim):
    angle = 1.0 / (10000.0 ** np.linspace(0.0, 1.0, dim // 2))
    angle = np.repeat(angle, 2)
    idx = f64(np.arange(length))
    angles = idx[:, None] * angle[None, :]
    return np.sin(angles), np.cos(angles)


def setup_inputs():
    s = mx_kscale(DM)
    X = bf(np.random.standard_normal((B, H, L, DM)) * s)
    q_words, q_scales = pack4(np.random.standard_normal((DM, DK)) * 3.0 / np.sqrt(DM) / s[:, None])
    k_words, k_scales = pack4(np.random.standard_normal((DM, DK)) * 3.0 / np.sqrt(DM) / s[:, None])
    return {"X": X,
            "W_Q_words": q_words, "W_Q_scales": q_scales,
            "W_K_words": k_words, "W_K_scales": k_scales}


def reference(X, W_Q_words, W_Q_scales, W_K_words, W_K_scales):
    xq = mxq(f64(X), 3, "e4m3")
    q = xq @ unpack4(W_Q_words, W_Q_scales)
    k = xq @ unpack4(W_K_words, W_K_scales)
    sin, cos = xpos_sincos(L, DK)
    q_rot = q * cos + rotate_every_two(q) * sin
    k_rot = k * cos + rotate_every_two(k) * (-sin)
    return (q_rot, k_rot)

@@ -1,0 +1,224 @@
+import math
+from contextlib import ExitStack
+
+import concourse.mybir as mybir
+from concourse.masks import make_identity
+
+F32 = mybir.dt.float32
+BF16 = mybir.dt.bfloat16
+I32 = mybir.dt.int32
+U32 = mybir.dt.uint32
+U8 = mybir.dt.uint8
+FP8X4 = mybir.dt.float8_e4m3fn_x4
+FP4X4 = mybir.dt.float4_e2m1fn_x4
+ALU = mybir.AluOpType
+ACT = mybir.ActivationFunctionType
+
+P = 128
+HEADS = 8
+K = 512
+DIM = 128
+PAIRS = DIM // 2
+ROWS = 8
+TILES = 4
+ROUNDS = HEADS * ROWS // TILES
+
+TWO_PI = 2.0 * math.pi
+ROPE_BASE = 10000.0
+ROUND_MAGIC = 12582912.0
+
+FLOPS = 2 * HEADS * 1024 * K * 2 * DIM
+
+
+def tile_retention_pa_t_kernel(
+    tc, X, W_Q_words, W_Q_scales, W_K_words, W_K_scales, out_0, out_1
+):
+    nc = tc.nc
+    x_rows = X.rearrange("b h (p j) k -> (b h) p j k", j=ROWS)
+    out_rows = [o.rearrange("b h (p j) d -> (b h) p j d", j=ROWS) for o in (out_0, out_1)]
+
+    with ExitStack() as ctx:
+        ctx.enter_context(tc.manual_schedule())
+        const = ctx.enter_context(tc.tile_pool(name="const", bufs=1))
+        x_pool = ctx.enter_context(tc.tile_pool(name="x", bufs=ROUNDS))
+        grouped_pool = ctx.enter_context(tc.tile_pool(name="grouped", bufs=3))
+        mx_pool = ctx.enter_context(tc.tile_pool(name="mx", bufs=3))
+        plane_pool = ctx.enter_context(tc.tile_pool(name="planes", bufs=3))
+        y_pool = ctx.enter_context(tc.tile_pool(name="y", bufs=6))
+        xt_pool = ctx.enter_context(tc.psum_pool(name="xt", bufs=4))
+        product_pool = ctx.enter_context(tc.psum_pool(name="product", bufs=4))
+
+        x_tiles = []
+
+        def load_x(r):
+            first = TILES * (r % 2)
+            x_sb = x_pool.tile([P, TILES, K], BF16, name="x_sb")
+            nc.sync.dma_start(out=x_sb[:], in_=x_rows[r // 2, :, first : first + TILES, :])
+            x_tiles.append(x_sb)
+
+        w_words = const.tile([P, 2, 2 * DIM], U8, align_bytes=64)
+        w_scales = const.tile([P, 2, DIM], U8, align_bytes=64)
+        nc.vector.memset(w_scales[:].bitcast(I32), 0)
+
+        load_x(0)
+        for w, (words, scales) in enumerate(((W_Q_words, W_Q_scales), (W_K_words, W_K_scales))):
+            nc.sync.dma_start(out=w_words[:, w, :].bitcast(I32), in_=words[0].bitcast(I32))
+            for quadrant in range(4):
+                nc.sync.dma_start(
+                    out=w_scales[32 * quadrant : 32 * quadrant + 4, w, :].bitcast(I32),
+                    in_=scales[0, 4 * quadrant : 4 * quadrant + 4, :].bitcast(I32),
+                )
+        for r in range(1, ROUNDS):
+            load_x(r)
+
+        warm = const.tile([P, 2], F32)
+        nc.vector.memset(warm[:], 0.0)
+        nc.scalar.activation(out=warm[:, 1:2], in_=warm[:, 0:1], func=ACT.Sin)
+
+        ident = const.tile([P, P], F32)
+        make_identity(nc, ident[:])
+
+        position = const.tile([P, ROWS], F32)
+        nc.gpsimd.iota(
+            position[:],
+            pattern=[[1, ROWS]],
+            base=0,
+            channel_multiplier=ROWS,
+            allow_small_or_imprecise_dtypes=True,
+        )
+        turns = const.tile([P, ROWS, PAIRS], F32)
+        nc.vector.tensor_scalar(
+            out=turns[:, :, 0:1],
+            in0=position[:].unsqueeze(2),
+            scalar1=1.0 / TWO_PI,
+            scalar2=None,
+            op0=ALU.mult,
+        )
+        for doubling in range(6):
+            n = 2**doubling
+            nc.vector.tensor_scalar(
+                out=turns[:, :, n : 2 * n],
+                in0=turns[:, :, 0:n],
+                scalar1=ROPE_BASE ** (-n / (PAIRS - 1)),
+                scalar2=None,
+                op0=ALU.mult,
+            )
+        whole = const.tile([P, ROWS, PAIRS], F32)
+        nc.vector.tensor_scalar(
+            out=whole[:],
+            in0=turns[:],
+            scalar1=ROUND_MAGIC,
+            scalar2=ROUND_MAGIC,
+            op0=ALU.add,
+            op1=ALU.subtract,
+        )
+        part = const.tile([P, ROWS, PAIRS], F32)
+        nc.vector.tensor_tensor(out=part[:], in0=turns[:], in1=whole[:], op=ALU.subtract)
+        size = const.tile([P, ROWS, PAIRS], F32)
+        nc.vector.scalar_tensor_tensor(
+            out=size[:], in0=part[:], scalar=-1.0, in1=part[:], op0=ALU.mult, op1=ALU.max
+        )
+        quarter_less = const.tile([P, ROWS, PAIRS], F32)
+        nc.vector.tensor_scalar(
+            out=quarter_less[:], in0=size[:], scalar1=-1.0, scalar2=0.25, op0=ALU.mult, op1=ALU.add
+        )
+
+        grouped_of = {}
+        products_of = {}
+
+        def transpose_and_regroup(r):
+            x_words = x_tiles[r][:].bitcast(F32)
+            grouped = grouped_pool.tile([P, TILES * K], BF16, name="grouped", align_bytes=64)
+            grouped_words = grouped[:].bitcast(F32).rearrange("p (t r u) -> p t r u", t=TILES, u=2)
+            for bank in range(TILES // 2):
+                xt = xt_pool.tile([P, 2, 2, P], F32, name="xt")
+                for t in range(2):
+                    for u in range(2):
+                        nc.tensor.transpose(
+                            out=xt[:, t, u, :],
+                            in_=x_words[:, 2 * bank + t, u : K // 2 : 2],
+                            identity=ident[:],
+                        )
+                nc.scalar.copy(
+                    out=grouped_words[:, 2 * bank : 2 * bank + 2, :, :],
+                    in_=xt[:].rearrange("p t u r -> p t r u"),
+                )
+            grouped_of[r] = grouped
+
+        def quantise_and_multiply(r):
+            codes = mx_pool.tile([P, TILES * P], U32, name="codes", align_bytes=64)
+            scales = mx_pool.tile([P, TILES * P], U8, name="scales", align_bytes=64)
+            nc.vector.quantize_mx(
+                out=codes[:].bitcast(FP8X4), scales=scales[:], in_=grouped_of[r][:]
+            )
+            products = []
+            for w in range(2):
+                product = product_pool.tile([P, TILES, DIM], F32, name="product")
+                for t in range(TILES):
+                    rows = slice(t * P, (t + 1) * P)
+                    nc.tensor.matmul_mx(
+                        out=product[:, t, :],
+                        lhsT=codes[:, rows].bitcast(FP8X4),
+                        lhsT_scale=scales[:, rows],
+                        rhs=w_words[:, w, :].bitcast(FP4X4),
+                        rhs_scale=w_scales[:, w, :],
+                        start=True,
+                        stop=True,
+                    )
+                products.append(product)
+            products_of[r] = products
+
+        def rotate_and_store(r):
+            first = TILES * (r % 2)
+            tiles = slice(first, first + TILES)
+            y = y_pool.tile([P, 2, TILES * DIM], F32, name="y")
+            planes = plane_pool.tile([P, 2, 2, TILES * PAIRS], F32, name="planes")
+            for w, product in enumerate(products_of[r]):
+                pairs = product[:].rearrange("p t (i e) -> p (t i) e", e=2)
+                for_even, for_odd = ((sin_minus, sin_plus), (sin_plus, sin_minus))[w]
+                nc.vector.tensor_tensor(
+                    out=planes[:, 0, w, :],
+                    in0=pairs[:, :, 1],
+                    in1=for_even[:, tiles, :].rearrange("p j i -> p (j i)"),
+                    op=ALU.mult,
+                )
+                nc.vector.tensor_tensor(
+                    out=planes[:, 1, w, :],
+                    in0=pairs[:, :, 0],
+                    in1=for_odd[:, tiles, :].rearrange("p j i -> p (j i)"),
+                    op=ALU.mult,
+                )
+                nc.vector.tensor_tensor(
+                    out=y[:, w, :].rearrange("p (n e) -> p n e", e=2),
+                    in0=pairs,
+                    in1=cos[:, tiles, :]
+                    .rearrange("p j i -> p (j i)")
+                    .unsqueeze(2)
+                    .to_broadcast([P, TILES * PAIRS, 2]),
+                    op=ALU.mult,
+                )
+            y_pairs = y[:].rearrange("p w (n e) -> p (w n) e", e=2)
+            nc.gpsimd.tensor_tensor(
+                out=y_pairs, in0=y_pairs, in1=planes[:].rearrange("p e w n -> p (w n) e"), op=ALU.add
+            )
+            for w in range(2):
+                nc.sync.dma_start(
+                    out=out_rows[w][r // 2, :, tiles, :],
+                    in_=y[:, w, :].rearrange("p (j d) -> p j d", d=DIM),
+                )
+
+        transpose_and_regroup(0)
+        sin_plus = const.tile([P, ROWS, PAIRS], F32)
+        sin_minus = const.tile([P, ROWS, PAIRS], F32)
+        cos = const.tile([P, ROWS, PAIRS], F32)
+        nc.scalar.activation(out=sin_plus[:], in_=part[:], func=ACT.Sin, scale=TWO_PI)
+        nc.scalar.activation(out=sin_minus[:], in_=part[:], func=ACT.Sin, scale=-TWO_PI)
+        nc.scalar.activation(out=cos[:], in_=quarter_less[:], func=ACT.Sin, scale=TWO_PI)
+
+        for r in range(ROUNDS):
+            if r + 1 < ROUNDS:
+                transpose_and_regroup(r + 1)
+            quantise_and_multiply(r)
+            if r >= 1:
+                rotate_and_store(r - 1)
+        rotate_and_store(ROUNDS - 1)

@@ -22,6 +22,7 @@ PAIRS = DIM // 2
 ROWS = 8
 TILES = 4
 ROUNDS = HEADS * ROWS // TILES
+VECTOR_ADDS_EVERY = 8
 
 TWO_PI = 2.0 * math.pi
 ROPE_BASE = 10000.0
@@ -43,8 +44,7 @@ def tile_retention_pa_t_kernel(
         x_pool = ctx.enter_context(tc.tile_pool(name="x", bufs=ROUNDS))
         grouped_pool = ctx.enter_context(tc.tile_pool(name="grouped", bufs=3))
         mx_pool = ctx.enter_context(tc.tile_pool(name="mx", bufs=3))
-        plane_pool = ctx.enter_context(tc.tile_pool(name="planes", bufs=3))
-        y_pool = ctx.enter_context(tc.tile_pool(name="y", bufs=6))
+        y_pool = ctx.enter_context(tc.tile_pool(name="y", bufs=5))
         xt_pool = ctx.enter_context(tc.psum_pool(name="xt", bufs=4))
         product_pool = ctx.enter_context(tc.psum_pool(name="product", bufs=4))
 
@@ -171,54 +171,40 @@ def tile_retention_pa_t_kernel(
         def rotate_and_store(r):
             first = TILES * (r % 2)
             tiles = slice(first, first + TILES)
-            y = y_pool.tile([P, 2, TILES * DIM], F32, name="y")
-            planes = plane_pool.tile([P, 2, 2, TILES * PAIRS], F32, name="planes")
+            y = y_pool.tile([P, 2, 2, TILES * DIM], F32, name="y")
             for w, product in enumerate(products_of[r]):
-                pairs = product[:].rearrange("p t (i e) -> p (t i) e", e=2)
-                for_even, for_odd = ((sin_minus, sin_plus), (sin_plus, sin_minus))[w]
-                nc.vector.tensor_tensor(
-                    out=planes[:, 0, w, :],
-                    in0=pairs[:, :, 1],
-                    in1=for_even[:, tiles, :].rearrange("p j i -> p (j i)"),
-                    op=ALU.mult,
+                factors = matrix[:, :, :, tiles, :].rearrange(
+                    ("p o s j i -> p s (j i) o", "p s o j i -> p s (j i) o")[w]
                 )
                 nc.vector.tensor_tensor(
-                    out=planes[:, 1, w, :],
-                    in0=pairs[:, :, 0],
-                    in1=for_odd[:, tiles, :].rearrange("p j i -> p (j i)"),
+                    out=y[:, w, :, :].rearrange("p s (n o) -> p s n o", o=2),
+                    in0=product[:]
+                    .rearrange("p t (i s) -> p s (t i)", s=2)
+                    .unsqueeze(3)
+                    .to_broadcast([P, 2, TILES * PAIRS, 2]),
+                    in1=factors,
                     op=ALU.mult,
                 )
-                nc.vector.tensor_tensor(
-                    out=y[:, w, :].rearrange("p (n e) -> p n e", e=2),
-                    in0=pairs,
-                    in1=cos[:, tiles, :]
-                    .rearrange("p j i -> p (j i)")
-                    .unsqueeze(2)
-                    .to_broadcast([P, TILES * PAIRS, 2]),
-                    op=ALU.mult,
-                )
-            y_pairs = y[:].rearrange("p w (n e) -> p (w n) e", e=2)
-            nc.gpsimd.tensor_tensor(
-                out=y_pairs, in0=y_pairs, in1=planes[:].rearrange("p e w n -> p (w n) e"), op=ALU.add
-            )
+            adder = nc.vector if r % VECTOR_ADDS_EVERY == VECTOR_ADDS_EVERY - 1 else nc.gpsimd
+            adder.tensor_tensor(out=y[:, :, 0, :], in0=y[:, :, 0, :], in1=y[:, :, 1, :], op=ALU.add)
             for w in range(2):
                 nc.sync.dma_start(
                     out=out_rows[w][r // 2, :, tiles, :],
-                    in_=y[:, w, :].rearrange("p (j d) -> p j d", d=DIM),
+                    in_=y[:, w, 0, :].rearrange("p (j d) -> p j d", d=DIM),
                 )
 
         transpose_and_regroup(0)
-        sin_plus = const.tile([P, ROWS, PAIRS], F32)
-        sin_minus = const.tile([P, ROWS, PAIRS], F32)
-        cos = const.tile([P, ROWS, PAIRS], F32)
-        nc.scalar.activation(out=sin_plus[:], in_=part[:], func=ACT.Sin, scale=TWO_PI)
-        nc.scalar.activation(out=sin_minus[:], in_=part[:], func=ACT.Sin, scale=-TWO_PI)
-        nc.scalar.activation(out=cos[:], in_=quarter_less[:], func=ACT.Sin, scale=TWO_PI)
+        transpose_and_regroup(1)
+        matrix = const.tile([P, 2, 2, ROWS, PAIRS], F32)
+        nc.scalar.activation(out=matrix[:, 0, 1, :, :], in_=part[:], func=ACT.Sin, scale=-TWO_PI)
+        nc.scalar.activation(out=matrix[:, 1, 0, :, :], in_=part[:], func=ACT.Sin, scale=TWO_PI)
+        nc.scalar.activation(out=matrix[:, 0, 0, :, :], in_=quarter_less[:], func=ACT.Sin, scale=TWO_PI)
+        nc.scalar.activation(out=matrix[:, 1, 1, :, :], in_=quarter_less[:], func=ACT.Sin, scale=TWO_PI)
 
+        quantise_and_multiply(0)
         for r in range(ROUNDS):
+            if r + 2 < ROUNDS:
+                transpose_and_regroup(r + 2)
             if r + 1 < ROUNDS:
-                transpose_and_regroup(r + 1)
-            quantise_and_multiply(r)
-            if r >= 1:
-                rotate_and_store(r - 1)
-        rotate_and_store(ROUNDS - 1)
+                quantise_and_multiply(r + 1)
+            rotate_and_store(r)

@@ -22,7 +22,6 @@ PAIRS = DIM // 2
 ROWS = 8
 TILES = 4
 ROUNDS = HEADS * ROWS // TILES
-VECTOR_ADDS_EVERY = 8
 
 TWO_PI = 2.0 * math.pi
 ROPE_BASE = 10000.0
@@ -61,22 +60,21 @@ def tile_retention_pa_t_kernel(
         nc.vector.memset(w_scales[:].bitcast(I32), 0)
 
         load_x(0)
-        for w, (words, scales) in enumerate(((W_Q_words, W_Q_scales), (W_K_words, W_K_scales))):
+        load_x(1)
+        for w, words in enumerate((W_Q_words, W_K_words)):
             nc.sync.dma_start(out=w_words[:, w, :].bitcast(I32), in_=words[0].bitcast(I32))
+        for w, scales in enumerate((W_Q_scales, W_K_scales)):
             for quadrant in range(4):
                 nc.sync.dma_start(
                     out=w_scales[32 * quadrant : 32 * quadrant + 4, w, :].bitcast(I32),
                     in_=scales[0, 4 * quadrant : 4 * quadrant + 4, :].bitcast(I32),
                 )
-        for r in range(1, ROUNDS):
+        for r in range(2, ROUNDS):
             load_x(r)
 
         warm = const.tile([P, 2], F32)
         nc.vector.memset(warm[:], 0.0)
         nc.scalar.activation(out=warm[:, 1:2], in_=warm[:, 0:1], func=ACT.Sin)
-
-        ident = const.tile([P, P], F32)
-        make_identity(nc, ident[:])
 
         position = const.tile([P, ROWS], F32)
         nc.gpsimd.iota(
@@ -86,6 +84,8 @@ def tile_retention_pa_t_kernel(
             channel_multiplier=ROWS,
             allow_small_or_imprecise_dtypes=True,
         )
+        ident = const.tile([P, P], F32)
+        make_identity(nc, ident[:])
         turns = const.tile([P, ROWS, PAIRS], F32)
         nc.vector.tensor_scalar(
             out=turns[:, :, 0:1],
@@ -185,7 +185,7 @@ def tile_retention_pa_t_kernel(
                     in1=factors,
                     op=ALU.mult,
                 )
-            adder = nc.vector if r % VECTOR_ADDS_EVERY == VECTOR_ADDS_EVERY - 1 else nc.gpsimd
+            adder = nc.vector if r == ROUNDS - 1 else nc.gpsimd
             adder.tensor_tensor(out=y[:, :, 0, :], in0=y[:, :, 0, :], in1=y[:, :, 1, :], op=ALU.add)
             for w in range(2):
                 nc.sync.dma_start(
@@ -193,15 +193,17 @@ def tile_retention_pa_t_kernel(
                     in_=y[:, w, 0, :].rearrange("p (j d) -> p j d", d=DIM),
                 )
 
-        transpose_and_regroup(0)
-        transpose_and_regroup(1)
         matrix = const.tile([P, 2, 2, ROWS, PAIRS], F32)
-        nc.scalar.activation(out=matrix[:, 0, 1, :, :], in_=part[:], func=ACT.Sin, scale=-TWO_PI)
+        transpose_and_regroup(0)
         nc.scalar.activation(out=matrix[:, 1, 0, :, :], in_=part[:], func=ACT.Sin, scale=TWO_PI)
         nc.scalar.activation(out=matrix[:, 0, 0, :, :], in_=quarter_less[:], func=ACT.Sin, scale=TWO_PI)
-        nc.scalar.activation(out=matrix[:, 1, 1, :, :], in_=quarter_less[:], func=ACT.Sin, scale=TWO_PI)
-
+        transpose_and_regroup(1)
         quantise_and_multiply(0)
+        nc.vector.tensor_scalar(
+            out=matrix[:, 0, 1, :, :], in0=matrix[:, 1, 0, :, :], scalar1=-1.0, scalar2=None, op0=ALU.mult
+        )
+        nc.vector.tensor_copy(out=matrix[:, 1, 1, :, :], in_=matrix[:, 0, 0, :, :])
+
         for r in range(ROUNDS):
             if r + 2 < ROUNDS:
                 transpose_and_regroup(r + 2)

@@ -43,9 +43,10 @@ def tile_retention_pa_t_kernel(
         x_pool = ctx.enter_context(tc.tile_pool(name="x", bufs=ROUNDS))
         grouped_pool = ctx.enter_context(tc.tile_pool(name="grouped", bufs=3))
         mx_pool = ctx.enter_context(tc.tile_pool(name="mx", bufs=3))
+        term_pool = ctx.enter_context(tc.tile_pool(name="term", bufs=3))
         y_pool = ctx.enter_context(tc.tile_pool(name="y", bufs=5))
-        xt_pool = ctx.enter_context(tc.psum_pool(name="xt", bufs=4))
-        product_pool = ctx.enter_context(tc.psum_pool(name="product", bufs=4))
+        xt_pool = ctx.enter_context(tc.psum_pool(name="xt", bufs=2))
+        product_pool = ctx.enter_context(tc.psum_pool(name="product", bufs=6))
 
         x_tiles = []
 
@@ -55,18 +56,20 @@ def tile_retention_pa_t_kernel(
             nc.sync.dma_start(out=x_sb[:], in_=x_rows[r // 2, :, first : first + TILES, :])
             x_tiles.append(x_sb)
 
-        w_words = const.tile([P, 2, 2 * DIM], U8, align_bytes=64)
-        w_scales = const.tile([P, 2, DIM], U8, align_bytes=64)
+        w_words = const.tile([P, 2 * 2 * DIM], U8, align_bytes=64)
+        w_scales = const.tile([P, 2 * DIM], U8, align_bytes=64)
         nc.vector.memset(w_scales[:].bitcast(I32), 0)
 
         load_x(0)
         load_x(1)
         for w, words in enumerate((W_Q_words, W_K_words)):
-            nc.sync.dma_start(out=w_words[:, w, :].bitcast(I32), in_=words[0].bitcast(I32))
+            nc.sync.dma_start(
+                out=w_words[:, 2 * DIM * w : 2 * DIM * (w + 1)].bitcast(I32), in_=words[0].bitcast(I32)
+            )
         for w, scales in enumerate((W_Q_scales, W_K_scales)):
             for quadrant in range(4):
                 nc.sync.dma_start(
-                    out=w_scales[32 * quadrant : 32 * quadrant + 4, w, :].bitcast(I32),
+                    out=w_scales[32 * quadrant : 32 * quadrant + 4, DIM * w : DIM * (w + 1)].bitcast(I32),
                     in_=scales[0, 4 * quadrant : 4 * quadrant + 4, :].bitcast(I32),
                 )
         for r in range(2, ROUNDS):
@@ -120,7 +123,7 @@ def tile_retention_pa_t_kernel(
         )
         quarter_less = const.tile([P, ROWS, PAIRS], F32)
         nc.vector.tensor_scalar(
-            out=quarter_less[:], in0=size[:], scalar1=-1.0, scalar2=0.25, op0=ALU.mult, op1=ALU.add
+            out=quarter_less[:], in0=size[:], scalar1=-0.25, scalar2=None, op0=ALU.add
         )
 
         grouped_of = {}
@@ -151,58 +154,90 @@ def tile_retention_pa_t_kernel(
             nc.vector.quantize_mx(
                 out=codes[:].bitcast(FP8X4), scales=scales[:], in_=grouped_of[r][:]
             )
-            products = []
-            for w in range(2):
-                product = product_pool.tile([P, TILES, DIM], F32, name="product")
-                for t in range(TILES):
-                    rows = slice(t * P, (t + 1) * P)
+            singles = [product_pool.tile([P, 2 * 2 * DIM], F32, name="product") for bank in range(TILES // 2)]
+            sums = product_pool.tile([P, TILES * DIM], F32, name="product")
+            for t in range(TILES):
+                rows = slice(t * P, (t + 1) * P)
+                nc.tensor.matmul_mx(
+                    out=singles[t // 2][:, 2 * DIM * (t % 2) : 2 * DIM * (t % 2 + 1)],
+                    lhsT=codes[:, rows].bitcast(FP8X4),
+                    lhsT_scale=scales[:, rows],
+                    rhs=split_words[:].bitcast(FP4X4),
+                    rhs_scale=split_scales[:],
+                    start=True,
+                    stop=True,
+                )
+                for o in range(2):
                     nc.tensor.matmul_mx(
-                        out=product[:, t, :],
+                        out=sums[:, DIM * t : DIM * (t + 1)],
                         lhsT=codes[:, rows].bitcast(FP8X4),
                         lhsT_scale=scales[:, rows],
-                        rhs=w_words[:, w, :].bitcast(FP4X4),
-                        rhs_scale=w_scales[:, w, :],
-                        start=True,
-                        stop=True,
+                        rhs=split_words[:, 2 * DIM * o : 2 * DIM * (o + 1)].bitcast(FP4X4),
+                        rhs_scale=split_scales[:, DIM * o : DIM * (o + 1)],
+                        start=(o == 0),
+                        stop=(o == 1),
                     )
-                products.append(product)
-            products_of[r] = products
+            products_of[r] = (singles, sums)
 
         def rotate_and_store(r):
             first = TILES * (r % 2)
             tiles = slice(first, first + TILES)
-            y = y_pool.tile([P, 2, 2, TILES * DIM], F32, name="y")
-            for w, product in enumerate(products_of[r]):
-                factors = matrix[:, :, :, tiles, :].rearrange(
-                    ("p o s j i -> p s (j i) o", "p s o j i -> p s (j i) o")[w]
-                )
+            singles, sums = products_of[r]
+            own = term_pool.tile([P, TILES * 2 * DIM], F32, name="own")
+            shared = term_pool.tile([P, TILES * DIM], F32, name="shared")
+            for bank in range(TILES // 2):
                 nc.vector.tensor_tensor(
-                    out=y[:, w, :, :].rearrange("p s (n o) -> p s n o", o=2),
-                    in0=product[:]
-                    .rearrange("p t (i s) -> p s (t i)", s=2)
-                    .unsqueeze(3)
-                    .to_broadcast([P, 2, TILES * PAIRS, 2]),
-                    in1=factors,
+                    out=own[:, 4 * DIM * bank : 4 * DIM * (bank + 1)],
+                    in0=singles[bank][:],
+                    in1=factors[:, 2 * DIM * (first + 2 * bank) : 2 * DIM * (first + 2 * bank + 2)],
                     op=ALU.mult,
                 )
+            nc.vector.tensor_tensor(
+                out=shared[:].rearrange("p (t w i) -> p t w i", w=2, i=PAIRS),
+                in0=sums[:].rearrange("p (t w i) -> p t w i", w=2, i=PAIRS),
+                in1=minus_cos[:, tiles, :].unsqueeze(2).to_broadcast([P, TILES, 2, PAIRS]),
+                op=ALU.mult,
+            )
             adder = nc.vector if r == ROUNDS - 1 else nc.gpsimd
-            adder.tensor_tensor(out=y[:, :, 0, :], in0=y[:, :, 0, :], in1=y[:, :, 1, :], op=ALU.add)
+            y = y_pool.tile([P, 2, TILES, DIM], F32, name="y")
+            own_by = own[:].rearrange("p (t o w i) -> p w t i o", o=2, w=2, i=PAIRS)
+            shared_by = shared[:].rearrange("p (t w i) -> p w t i", w=2, i=PAIRS)
             for w in range(2):
+                adder.tensor_tensor(
+                    out=y[:, w, :, :].rearrange("p t (i o) -> p t i o", o=2),
+                    in0=own_by[:, w, :, :, :],
+                    in1=shared_by[:, w, :, :].unsqueeze(3).to_broadcast([P, TILES, PAIRS, 2]),
+                    op=ALU.subtract,
+                )
                 nc.sync.dma_start(
                     out=out_rows[w][r // 2, :, tiles, :],
-                    in_=y[:, w, 0, :].rearrange("p (j d) -> p j d", d=DIM),
+                    in_=y[:, w, :, :],
                 )
 
-        matrix = const.tile([P, 2, 2, ROWS, PAIRS], F32)
+        split_words = const.tile([P, 2 * 2 * DIM], U8, align_bytes=64)
+        split_scales = const.tile([P, 2 * DIM], U8, align_bytes=64)
+        w_words_by = w_words[:].rearrange("p (n s b) -> p s n b", s=2, b=2)
+        w_scales_by = w_scales[:].rearrange("p (n s) -> p s n", s=2)
+        for o in range(2):
+            nc.vector.tensor_copy(
+                out=split_words[:, 2 * DIM * o : 2 * DIM * (o + 1)].rearrange("p (n b) -> p n b", b=2),
+                in_=w_words_by[:, 1 - o, :, :],
+            )
+            nc.vector.tensor_copy(out=split_scales[:, DIM * o : DIM * (o + 1)], in_=w_scales_by[:, 1 - o, :])
+
+        sine = const.tile([P, ROWS, PAIRS], F32)
+        minus_cos = const.tile([P, ROWS, PAIRS], F32)
+        factors = const.tile([P, ROWS * 2 * DIM], F32)
+        factors_by = factors[:].rearrange("p (j o w i) -> p o w j i", o=2, w=2, i=PAIRS)
         transpose_and_regroup(0)
-        nc.scalar.activation(out=matrix[:, 1, 0, :, :], in_=part[:], func=ACT.Sin, scale=TWO_PI)
-        nc.scalar.activation(out=matrix[:, 0, 0, :, :], in_=quarter_less[:], func=ACT.Sin, scale=TWO_PI)
+        nc.scalar.activation(out=sine[:], in_=part[:], func=ACT.Sin, scale=TWO_PI)
+        nc.scalar.activation(out=minus_cos[:], in_=quarter_less[:], func=ACT.Sin, scale=TWO_PI)
         transpose_and_regroup(1)
         quantise_and_multiply(0)
-        nc.vector.tensor_scalar(
-            out=matrix[:, 0, 1, :, :], in0=matrix[:, 1, 0, :, :], scalar1=-1.0, scalar2=None, op0=ALU.mult
-        )
-        nc.vector.tensor_copy(out=matrix[:, 1, 1, :, :], in_=matrix[:, 0, 0, :, :])
+        nc.vector.tensor_tensor(out=factors_by[:, 0, 0, :, :], in0=minus_cos[:], in1=sine[:], op=ALU.subtract)
+        nc.vector.tensor_tensor(out=factors_by[:, 0, 1, :, :], in0=minus_cos[:], in1=sine[:], op=ALU.add)
+        nc.vector.tensor_copy(out=factors_by[:, 1, 1, :, :], in_=factors_by[:, 0, 0, :, :])
+        nc.vector.tensor_copy(out=factors_by[:, 1, 0, :, :], in_=factors_by[:, 0, 1, :, :])
 
         for r in range(ROUNDS):
             if r + 2 < ROUNDS:

@@ -22,6 +22,7 @@ PAIRS = DIM // 2
 ROWS = 8
 TILES = 4
 ROUNDS = HEADS * ROWS // TILES
+GPSIMD_UNITS = 5
 
 TWO_PI = 2.0 * math.pi
 ROPE_BASE = 10000.0
@@ -179,39 +180,53 @@ def tile_retention_pa_t_kernel(
                     )
             products_of[r] = (singles, sums)
 
-        def rotate_and_store(r):
+        terms_of = {}
+
+        def multiply(r):
             first = TILES * (r % 2)
-            tiles = slice(first, first + TILES)
             singles, sums = products_of[r]
             own = term_pool.tile([P, TILES * 2 * DIM], F32, name="own")
             shared = term_pool.tile([P, TILES * DIM], F32, name="shared")
+            own_by = own[:].rearrange("p (c t i) -> p t c i", c=4, i=PAIRS)
             for bank in range(TILES // 2):
                 nc.vector.tensor_tensor(
-                    out=own[:, 4 * DIM * bank : 4 * DIM * (bank + 1)],
-                    in0=singles[bank][:],
-                    in1=factors[:, 2 * DIM * (first + 2 * bank) : 2 * DIM * (first + 2 * bank + 2)],
+                    out=own_by[:, 2 * bank : 2 * bank + 2, :, :],
+                    in0=singles[bank][:].rearrange("p (t c i) -> p t c i", c=4, i=PAIRS),
+                    in1=factors[:, 2 * DIM * (first + 2 * bank) : 2 * DIM * (first + 2 * bank + 2)].rearrange(
+                        "p (t c i) -> p t c i", c=4, i=PAIRS
+                    ),
                     op=ALU.mult,
                 )
             nc.vector.tensor_tensor(
-                out=shared[:].rearrange("p (t w i) -> p t w i", w=2, i=PAIRS),
+                out=shared[:].rearrange("p (w t i) -> p t w i", w=2, i=PAIRS),
                 in0=sums[:].rearrange("p (t w i) -> p t w i", w=2, i=PAIRS),
-                in1=minus_cos[:, tiles, :].unsqueeze(2).to_broadcast([P, TILES, 2, PAIRS]),
+                in1=minus_cos[:, first : first + TILES, :].unsqueeze(2).to_broadcast([P, TILES, 2, PAIRS]),
                 op=ALU.mult,
             )
-            adder = nc.vector if r == ROUNDS - 1 else nc.gpsimd
-            y = y_pool.tile([P, 2, TILES, DIM], F32, name="y")
-            own_by = own[:].rearrange("p (t o w i) -> p w t i o", o=2, w=2, i=PAIRS)
-            shared_by = shared[:].rearrange("p (t w i) -> p w t i", w=2, i=PAIRS)
+            terms_of[r] = (own, shared)
+
+        def subtract(engine, y, own, shared, n0, n1):
+            engine.tensor_tensor(
+                out=y[:, 2 * n0 : 2 * n1].rearrange("p (n o) -> p n o", o=2),
+                in0=own[:].rearrange("p (o n) -> p n o", o=2)[:, n0:n1, :],
+                in1=shared[:, n0:n1].unsqueeze(2).to_broadcast([P, n1 - n0, 2]),
+                op=ALU.subtract,
+            )
+
+        def add_and_store(r):
+            first = TILES * (r % 2)
+            own, shared = terms_of[r]
+            y = y_pool.tile([P, 2 * TILES * DIM], F32, name="y")
+            if r == ROUNDS - 1:
+                for w in range(2):
+                    subtract(nc.vector, y, own, shared, TILES * PAIRS * w, TILES * PAIRS * (w + 1))
+            else:
+                subtract(nc.vector, y, own, shared, GPSIMD_UNITS * PAIRS - 1, 2 * TILES * PAIRS)
+                subtract(nc.gpsimd, y, own, shared, 0, GPSIMD_UNITS * PAIRS)
             for w in range(2):
-                adder.tensor_tensor(
-                    out=y[:, w, :, :].rearrange("p t (i o) -> p t i o", o=2),
-                    in0=own_by[:, w, :, :, :],
-                    in1=shared_by[:, w, :, :].unsqueeze(3).to_broadcast([P, TILES, PAIRS, 2]),
-                    op=ALU.subtract,
-                )
                 nc.sync.dma_start(
-                    out=out_rows[w][r // 2, :, tiles, :],
-                    in_=y[:, w, :, :],
+                    out=out_rows[w][r // 2, :, first : first + TILES, :],
+                    in_=y[:, TILES * DIM * w : TILES * DIM * (w + 1)].rearrange("p (j d) -> p j d", d=DIM),
                 )
 
         split_words = const.tile([P, 2 * 2 * DIM], U8, align_bytes=64)
@@ -244,4 +259,7 @@ def tile_retention_pa_t_kernel(
                 transpose_and_regroup(r + 2)
             if r + 1 < ROUNDS:
                 quantise_and_multiply(r + 1)
-            rotate_and_store(r)
+            if r > 0:
+                add_and_store(r - 1)
+            multiply(r)
+        add_and_store(ROUNDS - 1)

@@ -22,7 +22,7 @@ PAIRS = DIM // 2
 ROWS = 8
 TILES = 4
 ROUNDS = HEADS * ROWS // TILES
-GPSIMD_UNITS = 5
+GPSIMD_UNITS = 4
 
 TWO_PI = 2.0 * math.pi
 ROPE_BASE = 10000.0

@@ -51,34 +51,51 @@ def tile_retention_pa_t_kernel(
 
         x_tiles = []
 
-        def load_x(r):
+        def load_x(r, t0=0, t1=TILES):
+            if t0 == 0:
+                x_tiles.append(x_pool.tile([P, TILES, K], BF16, name="x_sb"))
             first = TILES * (r % 2)
-            x_sb = x_pool.tile([P, TILES, K], BF16, name="x_sb")
-            nc.sync.dma_start(out=x_sb[:], in_=x_rows[r // 2, :, first : first + TILES, :])
-            x_tiles.append(x_sb)
+            nc.sync.dma_start(
+                out=x_tiles[r][:, t0:t1, :], in_=x_rows[r // 2, :, first + t0 : first + t1, :]
+            )
 
         w_words = const.tile([P, 2 * 2 * DIM], U8, align_bytes=64)
         w_scales = const.tile([P, 2 * DIM], U8, align_bytes=64)
         nc.vector.memset(w_scales[:].bitcast(I32), 0)
 
-        load_x(0)
-        load_x(1)
-        for w, words in enumerate((W_Q_words, W_K_words)):
+        def load_words(w, words):
             nc.sync.dma_start(
                 out=w_words[:, 2 * DIM * w : 2 * DIM * (w + 1)].bitcast(I32), in_=words[0].bitcast(I32)
             )
-        for w, scales in enumerate((W_Q_scales, W_K_scales)):
+
+        def load_scales(w, scales):
             for quadrant in range(4):
                 nc.sync.dma_start(
                     out=w_scales[32 * quadrant : 32 * quadrant + 4, DIM * w : DIM * (w + 1)].bitcast(I32),
                     in_=scales[0, 4 * quadrant : 4 * quadrant + 4, :].bitcast(I32),
                 )
+
+        load_x(0, 0, TILES // 2)
+        load_scales(0, W_Q_scales)
+        load_words(0, W_Q_words)
+        load_x(0, TILES // 2, TILES)
+        load_x(1)
+        load_words(1, W_K_words)
+        load_scales(1, W_K_scales)
         for r in range(2, ROUNDS):
             load_x(r)
 
         warm = const.tile([P, 2], F32)
         nc.vector.memset(warm[:], 0.0)
         nc.scalar.activation(out=warm[:, 1:2], in_=warm[:, 0:1], func=ACT.Sin)
+
+        zeros = const.tile([P, 4 * P], BF16)
+        nc.vector.memset(zeros[:], 0.0)
+
+        def keep_warm(count):
+            idle = product_pool.tile([P, 4 * P], F32, name="product")
+            for n in range(count):
+                nc.tensor.matmul(out=idle[:], lhsT=zeros[:, 0:P], rhs=zeros[:], start=True, stop=True)
 
         position = const.tile([P, ROWS], F32)
         nc.gpsimd.iota(
@@ -91,41 +108,37 @@ def tile_retention_pa_t_kernel(
         ident = const.tile([P, P], F32)
         make_identity(nc, ident[:])
         turns = const.tile([P, ROWS, PAIRS], F32)
-        nc.vector.tensor_scalar(
-            out=turns[:, :, 0:1],
-            in0=position[:].unsqueeze(2),
-            scalar1=1.0 / TWO_PI,
-            scalar2=None,
-            op0=ALU.mult,
-        )
-        for doubling in range(6):
-            n = 2**doubling
+        for i in range(4):
             nc.vector.tensor_scalar(
-                out=turns[:, :, n : 2 * n],
-                in0=turns[:, :, 0:n],
-                scalar1=ROPE_BASE ** (-n / (PAIRS - 1)),
+                out=turns[:, :, i : i + 1],
+                in0=position[:].unsqueeze(2),
+                scalar1=ROPE_BASE ** (-i / (PAIRS - 1)) / TWO_PI,
                 scalar2=None,
                 op0=ALU.mult,
             )
-        whole = const.tile([P, ROWS, PAIRS], F32)
+        for n in (4, 16):
+            for part_of_four in range(1, 4):
+                nc.vector.tensor_scalar(
+                    out=turns[:, :, n * part_of_four : n * (part_of_four + 1)],
+                    in0=turns[:, :, 0:n],
+                    scalar1=ROPE_BASE ** (-n * part_of_four / (PAIRS - 1)),
+                    scalar2=None,
+                    op0=ALU.mult,
+                )
+        shifted = const.tile([P, ROWS, PAIRS], F32)
         nc.vector.tensor_scalar(
-            out=whole[:],
-            in0=turns[:],
-            scalar1=ROUND_MAGIC,
-            scalar2=ROUND_MAGIC,
-            op0=ALU.add,
-            op1=ALU.subtract,
+            out=shifted[:], in0=turns[:], scalar1=ROUND_MAGIC, scalar2=None, op0=ALU.add
+        )
+        shifted_cos = const.tile([P, ROWS, PAIRS], F32)
+        nc.vector.tensor_scalar(
+            out=shifted_cos[:], in0=turns[:], scalar1=0.25, scalar2=ROUND_MAGIC, op0=ALU.add, op1=ALU.add
         )
         part = const.tile([P, ROWS, PAIRS], F32)
-        nc.vector.tensor_tensor(out=part[:], in0=turns[:], in1=whole[:], op=ALU.subtract)
-        size = const.tile([P, ROWS, PAIRS], F32)
-        nc.vector.scalar_tensor_tensor(
-            out=size[:], in0=part[:], scalar=-1.0, in1=part[:], op0=ALU.mult, op1=ALU.max
-        )
-        quarter_less = const.tile([P, ROWS, PAIRS], F32)
-        nc.vector.tensor_scalar(
-            out=quarter_less[:], in0=size[:], scalar1=-0.25, scalar2=None, op0=ALU.add
-        )
+        part_cos = const.tile([P, ROWS, PAIRS], F32)
+        for out, whole in ((part, shifted), (part_cos, shifted_cos)):
+            nc.vector.scalar_tensor_tensor(
+                out=out[:], in0=whole[:], scalar=ROUND_MAGIC, in1=turns[:], op0=ALU.subtract, op1=ALU.subtract
+            )
 
         grouped_of = {}
         products_of = {}
@@ -233,26 +246,46 @@ def tile_retention_pa_t_kernel(
         split_scales = const.tile([P, 2 * DIM], U8, align_bytes=64)
         w_words_by = w_words[:].rearrange("p (n s b) -> p s n b", s=2, b=2)
         w_scales_by = w_scales[:].rearrange("p (n s) -> p s n", s=2)
+        sine = const.tile([P, ROWS, PAIRS], F32)
+        minus_cos = const.tile([P, ROWS, PAIRS], F32)
+        factors = const.tile([P, ROWS * 2 * DIM], F32)
+        factors_by = factors[:].rearrange("p (j o w i) -> p o w j i", o=2, w=2, i=PAIRS)
+
+        def sine_and_cosine(first):
+            js = slice(first, first + TILES)
+            nc.scalar.activation(out=sine[:, js, :], in_=part[:, js, :], func=ACT.Sin, scale=-TWO_PI)
+            nc.scalar.activation(
+                out=minus_cos[:, js, :], in_=part_cos[:, js, :], func=ACT.Sin, scale=TWO_PI, bias=-0.5 * math.pi
+            )
+
+        def fill_factors(first):
+            js = slice(first, first + TILES)
+            nc.vector.tensor_tensor(
+                out=factors_by[:, 0, 0, js, :], in0=minus_cos[:, js, :], in1=sine[:, js, :], op=ALU.subtract
+            )
+            nc.vector.tensor_tensor(
+                out=factors_by[:, 0, 1, js, :], in0=minus_cos[:, js, :], in1=sine[:, js, :], op=ALU.add
+            )
+            nc.vector.tensor_copy(out=factors_by[:, 1, 1, js, :], in_=factors_by[:, 0, 0, js, :])
+            nc.vector.tensor_copy(out=factors_by[:, 1, 0, js, :], in_=factors_by[:, 0, 1, js, :])
+
+        keep_warm(5)
+        sine_and_cosine(0)
+        fill_factors(0)
+        transpose_and_regroup(0)
+        keep_warm(2)
+        sine_and_cosine(TILES)
+        transpose_and_regroup(1)
+        keep_warm(1)
         for o in range(2):
             nc.vector.tensor_copy(
                 out=split_words[:, 2 * DIM * o : 2 * DIM * (o + 1)].rearrange("p (n b) -> p n b", b=2),
                 in_=w_words_by[:, 1 - o, :, :],
             )
+        for o in range(2):
             nc.vector.tensor_copy(out=split_scales[:, DIM * o : DIM * (o + 1)], in_=w_scales_by[:, 1 - o, :])
-
-        sine = const.tile([P, ROWS, PAIRS], F32)
-        minus_cos = const.tile([P, ROWS, PAIRS], F32)
-        factors = const.tile([P, ROWS * 2 * DIM], F32)
-        factors_by = factors[:].rearrange("p (j o w i) -> p o w j i", o=2, w=2, i=PAIRS)
-        transpose_and_regroup(0)
-        nc.scalar.activation(out=sine[:], in_=part[:], func=ACT.Sin, scale=TWO_PI)
-        nc.scalar.activation(out=minus_cos[:], in_=quarter_less[:], func=ACT.Sin, scale=TWO_PI)
-        transpose_and_regroup(1)
         quantise_and_multiply(0)
-        nc.vector.tensor_tensor(out=factors_by[:, 0, 0, :, :], in0=minus_cos[:], in1=sine[:], op=ALU.subtract)
-        nc.vector.tensor_tensor(out=factors_by[:, 0, 1, :, :], in0=minus_cos[:], in1=sine[:], op=ALU.add)
-        nc.vector.tensor_copy(out=factors_by[:, 1, 1, :, :], in_=factors_by[:, 0, 0, :, :])
-        nc.vector.tensor_copy(out=factors_by[:, 1, 0, :, :], in_=factors_by[:, 0, 1, :, :])
+        fill_factors(TILES)
 
         for r in range(ROUNDS):
             if r + 2 < ROUNDS:

@@ -22,7 +22,7 @@ PAIRS = DIM // 2
 ROWS = 8
 TILES = 4
 ROUNDS = HEADS * ROWS // TILES
-GPSIMD_UNITS = 4
+GPSIMD_UNITS = 5
 
 TWO_PI = 2.0 * math.pi
 ROPE_BASE = 10000.0
@@ -42,7 +42,7 @@ def tile_retention_pa_t_kernel(
         ctx.enter_context(tc.manual_schedule())
         const = ctx.enter_context(tc.tile_pool(name="const", bufs=1))
         x_pool = ctx.enter_context(tc.tile_pool(name="x", bufs=ROUNDS))
-        grouped_pool = ctx.enter_context(tc.tile_pool(name="grouped", bufs=3))
+        grouped_pool = ctx.enter_context(tc.tile_pool(name="grouped", bufs=4))
         mx_pool = ctx.enter_context(tc.tile_pool(name="mx", bufs=3))
         term_pool = ctx.enter_context(tc.tile_pool(name="term", bufs=3))
         y_pool = ctx.enter_context(tc.tile_pool(name="y", bufs=5))
@@ -68,20 +68,21 @@ def tile_retention_pa_t_kernel(
                 out=w_words[:, 2 * DIM * w : 2 * DIM * (w + 1)].bitcast(I32), in_=words[0].bitcast(I32)
             )
 
-        def load_scales(w, scales):
-            for quadrant in range(4):
+        def load_scales(w, scales, quadrants):
+            for quadrant in quadrants:
                 nc.sync.dma_start(
                     out=w_scales[32 * quadrant : 32 * quadrant + 4, DIM * w : DIM * (w + 1)].bitcast(I32),
                     in_=scales[0, 4 * quadrant : 4 * quadrant + 4, :].bitcast(I32),
                 )
 
         load_x(0, 0, TILES // 2)
-        load_scales(0, W_Q_scales)
         load_words(0, W_Q_words)
-        load_x(0, TILES // 2, TILES)
-        load_x(1)
         load_words(1, W_K_words)
-        load_scales(1, W_K_scales)
+        load_x(0, TILES // 2, TILES)
+        load_scales(0, W_Q_scales, range(3))
+        load_x(1)
+        load_scales(0, W_Q_scales, range(3, 4))
+        load_scales(1, W_K_scales, range(4))
         for r in range(2, ROUNDS):
             load_x(r)
 
@@ -90,7 +91,6 @@ def tile_retention_pa_t_kernel(
         nc.scalar.activation(out=warm[:, 1:2], in_=warm[:, 0:1], func=ACT.Sin)
 
         zeros = const.tile([P, 4 * P], BF16)
-        nc.vector.memset(zeros[:], 0.0)
 
         def keep_warm(count):
             idle = product_pool.tile([P, 4 * P], F32, name="product")
@@ -105,6 +105,7 @@ def tile_retention_pa_t_kernel(
             channel_multiplier=ROWS,
             allow_small_or_imprecise_dtypes=True,
         )
+        nc.gpsimd.memset(zeros[:], 0.0)
         ident = const.tile([P, P], F32)
         make_identity(nc, ident[:])
         turns = const.tile([P, ROWS, PAIRS], F32)
@@ -129,16 +130,18 @@ def tile_retention_pa_t_kernel(
         nc.vector.tensor_scalar(
             out=shifted[:], in0=turns[:], scalar1=ROUND_MAGIC, scalar2=None, op0=ALU.add
         )
-        shifted_cos = const.tile([P, ROWS, PAIRS], F32)
-        nc.vector.tensor_scalar(
-            out=shifted_cos[:], in0=turns[:], scalar1=0.25, scalar2=ROUND_MAGIC, op0=ALU.add, op1=ALU.add
-        )
         part = const.tile([P, ROWS, PAIRS], F32)
-        part_cos = const.tile([P, ROWS, PAIRS], F32)
-        for out, whole in ((part, shifted), (part_cos, shifted_cos)):
+        for first in range(0, ROWS, TILES):
+            js = slice(first, first + TILES)
             nc.vector.scalar_tensor_tensor(
-                out=out[:], in0=whole[:], scalar=ROUND_MAGIC, in1=turns[:], op0=ALU.subtract, op1=ALU.subtract
+                out=part[:, js, :],
+                in0=shifted[:, js, :],
+                scalar=ROUND_MAGIC,
+                in1=turns[:, js, :],
+                op0=ALU.subtract,
+                op1=ALU.subtract,
             )
+        size = const.tile([P, ROWS, PAIRS], F32)
 
         grouped_of = {}
         products_of = {}
@@ -162,12 +165,18 @@ def tile_retention_pa_t_kernel(
                 )
             grouped_of[r] = grouped
 
-        def quantise_and_multiply(r):
+        quantised_of = {}
+
+        def quantise(r):
             codes = mx_pool.tile([P, TILES * P], U32, name="codes", align_bytes=64)
             scales = mx_pool.tile([P, TILES * P], U8, name="scales", align_bytes=64)
             nc.vector.quantize_mx(
                 out=codes[:].bitcast(FP8X4), scales=scales[:], in_=grouped_of[r][:]
             )
+            quantised_of[r] = (codes, scales)
+
+        def multiply_by_weights(r):
+            codes, scales = quantised_of[r]
             singles = [product_pool.tile([P, 2 * 2 * DIM], F32, name="product") for bank in range(TILES // 2)]
             sums = product_pool.tile([P, TILES * DIM], F32, name="product")
             for t in range(TILES):
@@ -176,11 +185,13 @@ def tile_retention_pa_t_kernel(
                     out=singles[t // 2][:, 2 * DIM * (t % 2) : 2 * DIM * (t % 2 + 1)],
                     lhsT=codes[:, rows].bitcast(FP8X4),
                     lhsT_scale=scales[:, rows],
-                    rhs=split_words[:].bitcast(FP4X4),
-                    rhs_scale=split_scales[:],
+                    rhs=w_words[:].bitcast(FP4X4),
+                    rhs_scale=w_scales[:],
                     start=True,
                     stop=True,
                 )
+            for t in range(TILES):
+                rows = slice(t * P, (t + 1) * P)
                 for o in range(2):
                     nc.tensor.matmul_mx(
                         out=sums[:, DIM * t : DIM * (t + 1)],
@@ -200,99 +211,143 @@ def tile_retention_pa_t_kernel(
             singles, sums = products_of[r]
             own = term_pool.tile([P, TILES * 2 * DIM], F32, name="own")
             shared = term_pool.tile([P, TILES * DIM], F32, name="shared")
-            own_by = own[:].rearrange("p (c t i) -> p t c i", c=4, i=PAIRS)
+            own_by = own[:].rearrange("p (w t d) -> p t w d", w=2, d=DIM)
+            def multiply_sums():
+                nc.vector.tensor_tensor(
+                    out=shared[:].rearrange("p (w t i) -> p t w i", w=2, i=PAIRS),
+                    in0=sums[:].rearrange("p (t w i) -> p t w i", w=2, i=PAIRS),
+                    in1=minus_cos[:, first : first + TILES, :].unsqueeze(2).to_broadcast([P, TILES, 2, PAIRS]),
+                    op=ALU.mult,
+                )
+
+            if r == ROUNDS - 1:
+                multiply_sums()
             for bank in range(TILES // 2):
+                if r == 0 and bank == 1:
+                    fill_factors(TILES)
                 nc.vector.tensor_tensor(
                     out=own_by[:, 2 * bank : 2 * bank + 2, :, :],
-                    in0=singles[bank][:].rearrange("p (t c i) -> p t c i", c=4, i=PAIRS),
+                    in0=singles[bank][:].rearrange("p (t w d) -> p t w d", w=2, d=DIM),
                     in1=factors[:, 2 * DIM * (first + 2 * bank) : 2 * DIM * (first + 2 * bank + 2)].rearrange(
-                        "p (t c i) -> p t c i", c=4, i=PAIRS
+                        "p (t w d) -> p t w d", w=2, d=DIM
                     ),
                     op=ALU.mult,
                 )
-            nc.vector.tensor_tensor(
-                out=shared[:].rearrange("p (w t i) -> p t w i", w=2, i=PAIRS),
-                in0=sums[:].rearrange("p (t w i) -> p t w i", w=2, i=PAIRS),
-                in1=minus_cos[:, first : first + TILES, :].unsqueeze(2).to_broadcast([P, TILES, 2, PAIRS]),
-                op=ALU.mult,
-            )
+            if r < ROUNDS - 1:
+                multiply_sums()
             terms_of[r] = (own, shared)
 
         def subtract(engine, y, own, shared, n0, n1):
             engine.tensor_tensor(
                 out=y[:, 2 * n0 : 2 * n1].rearrange("p (n o) -> p n o", o=2),
-                in0=own[:].rearrange("p (o n) -> p n o", o=2)[:, n0:n1, :],
+                in0=own[:].rearrange("p (n s) -> p n s", s=2)[:, n0:n1, ::-1],
                 in1=shared[:, n0:n1].unsqueeze(2).to_broadcast([P, n1 - n0, 2]),
                 op=ALU.subtract,
             )
 
-        def add_and_store(r):
+        def store(r, w, t0, t1, y_rows):
             first = TILES * (r % 2)
+            nc.sync.dma_start(
+                out=out_rows[w][r // 2, :, first + t0 : first + t1, :],
+                in_=y_rows.rearrange("p (j d) -> p j d", d=DIM),
+            )
+
+        def add_and_store(r):
             own, shared = terms_of[r]
             y = y_pool.tile([P, 2 * TILES * DIM], F32, name="y")
-            if r == ROUNDS - 1:
-                for w in range(2):
-                    subtract(nc.vector, y, own, shared, TILES * PAIRS * w, TILES * PAIRS * (w + 1))
-            else:
-                subtract(nc.vector, y, own, shared, GPSIMD_UNITS * PAIRS - 1, 2 * TILES * PAIRS)
-                subtract(nc.gpsimd, y, own, shared, 0, GPSIMD_UNITS * PAIRS)
+            subtract(nc.vector, y, own, shared, GPSIMD_UNITS * PAIRS - 1, 2 * TILES * PAIRS)
+            subtract(nc.gpsimd, y, own, shared, 0, GPSIMD_UNITS * PAIRS)
             for w in range(2):
-                nc.sync.dma_start(
-                    out=out_rows[w][r // 2, :, first : first + TILES, :],
-                    in_=y[:, TILES * DIM * w : TILES * DIM * (w + 1)].rearrange("p (j d) -> p j d", d=DIM),
+                store(r, w, 0, TILES, y[:, TILES * DIM * w : TILES * DIM * (w + 1)])
+
+        def add_and_store_last(r):
+            own, shared = terms_of[r]
+            for t0, t1 in ((0, 2), (2, 3), (3, 4)):
+                width = DIM * (t1 - t0)
+                y = y_pool.tile([P, 2 * width], F32, name="y")
+                n = slice(PAIRS * t0, PAIRS * t1)
+                nc.vector.tensor_tensor(
+                    out=y[:].rearrange("p (w n o) -> p w n o", w=2, o=2),
+                    in0=own[:].rearrange("p (w n s) -> p w n s", w=2, s=2)[:, :, n, ::-1],
+                    in1=shared[:]
+                    .rearrange("p (w n) -> p w n", w=2)[:, :, n]
+                    .unsqueeze(3)
+                    .to_broadcast([P, 2, PAIRS * (t1 - t0), 2]),
+                    op=ALU.subtract,
                 )
+                for w in range(2):
+                    store(r, w, t0, t1, y[:, width * w : width * (w + 1)])
 
         split_words = const.tile([P, 2 * 2 * DIM], U8, align_bytes=64)
         split_scales = const.tile([P, 2 * DIM], U8, align_bytes=64)
         w_words_by = w_words[:].rearrange("p (n s b) -> p s n b", s=2, b=2)
         w_scales_by = w_scales[:].rearrange("p (n s) -> p s n", s=2)
-        sine = const.tile([P, ROWS, PAIRS], F32)
+        sines = const.tile([P, 2, ROWS, PAIRS], F32)
         minus_cos = const.tile([P, ROWS, PAIRS], F32)
         factors = const.tile([P, ROWS * 2 * DIM], F32)
-        factors_by = factors[:].rearrange("p (j o w i) -> p o w j i", o=2, w=2, i=PAIRS)
+        factors_by = factors[:].rearrange("p (j w i s) -> p w j i s", w=2, i=PAIRS, s=2)
 
         def sine_and_cosine(first):
             js = slice(first, first + TILES)
-            nc.scalar.activation(out=sine[:, js, :], in_=part[:, js, :], func=ACT.Sin, scale=-TWO_PI)
+            nc.scalar.activation(out=size[:, js, :], in_=part[:, js, :], func=ACT.Abs)
+            for n, sign in enumerate((-1.0, 1.0)):
+                nc.scalar.activation(
+                    out=sines[:, n, js, :], in_=part[:, js, :], func=ACT.Sin, scale=sign * TWO_PI
+                )
             nc.scalar.activation(
-                out=minus_cos[:, js, :], in_=part_cos[:, js, :], func=ACT.Sin, scale=TWO_PI, bias=-0.5 * math.pi
+                out=minus_cos[:, js, :], in_=size[:, js, :], func=ACT.Sin, scale=TWO_PI, bias=-0.5 * math.pi
             )
 
         def fill_factors(first):
             js = slice(first, first + TILES)
             nc.vector.tensor_tensor(
-                out=factors_by[:, 0, 0, js, :], in0=minus_cos[:, js, :], in1=sine[:, js, :], op=ALU.subtract
+                out=factors_by[:, 0, js, :, :],
+                in0=minus_cos[:, js, :].unsqueeze(3).to_broadcast([P, TILES, PAIRS, 2]),
+                in1=sines[:, :, js, :].rearrange("p s j i -> p j i s"),
+                op=ALU.add,
             )
-            nc.vector.tensor_tensor(
-                out=factors_by[:, 0, 1, js, :], in0=minus_cos[:, js, :], in1=sine[:, js, :], op=ALU.add
-            )
-            nc.vector.tensor_copy(out=factors_by[:, 1, 1, js, :], in_=factors_by[:, 0, 0, js, :])
-            nc.vector.tensor_copy(out=factors_by[:, 1, 0, js, :], in_=factors_by[:, 0, 1, js, :])
+            if first == 0:
+                nc.vector.tensor_tensor(
+                    out=factors_by[:, 1, js, :, :],
+                    in0=minus_cos[:, js, :].unsqueeze(3).to_broadcast([P, TILES, PAIRS, 2]),
+                    in1=sines[:, :, js, :].rearrange("p s j i -> p j i s"),
+                    op=ALU.subtract,
+                )
+            else:
+                nc.gpsimd.tensor_scalar(
+                    out=factors_by[:, 1, js, :, :],
+                    in0=factors_by[:, 0, js, :, ::-1],
+                    scalar1=1.0,
+                    scalar2=0.0,
+                    op0=ALU.mult,
+                    op1=ALU.add,
+                )
 
-        keep_warm(5)
-        sine_and_cosine(0)
-        fill_factors(0)
-        transpose_and_regroup(0)
-        keep_warm(2)
-        sine_and_cosine(TILES)
-        transpose_and_regroup(1)
-        keep_warm(1)
         for o in range(2):
             nc.vector.tensor_copy(
                 out=split_words[:, 2 * DIM * o : 2 * DIM * (o + 1)].rearrange("p (n b) -> p n b", b=2),
                 in_=w_words_by[:, 1 - o, :, :],
             )
+        keep_warm(5)
+        sine_and_cosine(0)
+        fill_factors(0)
+        transpose_and_regroup(0)
+        keep_warm(2)
+        transpose_and_regroup(1)
+        sine_and_cosine(TILES)
+        keep_warm(1)
+        quantise(0)
         for o in range(2):
             nc.vector.tensor_copy(out=split_scales[:, DIM * o : DIM * (o + 1)], in_=w_scales_by[:, 1 - o, :])
-        quantise_and_multiply(0)
-        fill_factors(TILES)
+        multiply_by_weights(0)
 
         for r in range(ROUNDS):
             if r + 2 < ROUNDS:
                 transpose_and_regroup(r + 2)
             if r + 1 < ROUNDS:
-                quantise_and_multiply(r + 1)
+                quantise(r + 1)
+                multiply_by_weights(r + 1)
             if r > 0:
                 add_and_store(r - 1)
             multiply(r)
-        add_and_store(ROUNDS - 1)
+        add_and_store_last(ROUNDS - 1)

@@ -22,7 +22,7 @@ PAIRS = DIM // 2
 ROWS = 8
 TILES = 4
 ROUNDS = HEADS * ROWS // TILES
-GPSIMD_UNITS = 5
+GPSIMD_PAIRS = 288
 
 TWO_PI = 2.0 * math.pi
 ROPE_BASE = 10000.0
@@ -255,8 +255,8 @@ def tile_retention_pa_t_kernel(
         def add_and_store(r):
             own, shared = terms_of[r]
             y = y_pool.tile([P, 2 * TILES * DIM], F32, name="y")
-            subtract(nc.vector, y, own, shared, GPSIMD_UNITS * PAIRS - 1, 2 * TILES * PAIRS)
-            subtract(nc.gpsimd, y, own, shared, 0, GPSIMD_UNITS * PAIRS)
+            subtract(nc.vector, y, own, shared, GPSIMD_PAIRS - 1, 2 * TILES * PAIRS)
+            subtract(nc.gpsimd, y, own, shared, 0, GPSIMD_PAIRS)
             for w in range(2):
                 store(r, w, 0, TILES, y[:, TILES * DIM * w : TILES * DIM * (w + 1)])
 

@@ -22,7 +22,7 @@ PAIRS = DIM // 2
 ROWS = 8
 TILES = 4
 ROUNDS = HEADS * ROWS // TILES
-GPSIMD_PAIRS = 288
+GPSIMD_PAIRS = 304
 
 TWO_PI = 2.0 * math.pi
 ROPE_BASE = 10000.0
@@ -131,6 +131,7 @@ def tile_retention_pa_t_kernel(
             out=shifted[:], in0=turns[:], scalar1=ROUND_MAGIC, scalar2=None, op0=ALU.add
         )
         part = const.tile([P, ROWS, PAIRS], F32)
+        size = const.tile([P, ROWS, PAIRS], F32)
         for first in range(0, ROWS, TILES):
             js = slice(first, first + TILES)
             nc.vector.scalar_tensor_tensor(
@@ -141,7 +142,16 @@ def tile_retention_pa_t_kernel(
                 op0=ALU.subtract,
                 op1=ALU.subtract,
             )
-        size = const.tile([P, ROWS, PAIRS], F32)
+        for first in range(0, ROWS, TILES):
+            js = slice(first, first + TILES)
+            nc.vector.scalar_tensor_tensor(
+                out=size[:, js, :],
+                in0=part[:, js, :],
+                scalar=-1.0,
+                in1=part[:, js, :],
+                op0=ALU.mult,
+                op1=ALU.max,
+            )
 
         grouped_of = {}
         products_of = {}
@@ -185,8 +195,8 @@ def tile_retention_pa_t_kernel(
                     out=singles[t // 2][:, 2 * DIM * (t % 2) : 2 * DIM * (t % 2 + 1)],
                     lhsT=codes[:, rows].bitcast(FP8X4),
                     lhsT_scale=scales[:, rows],
-                    rhs=w_words[:].bitcast(FP4X4),
-                    rhs_scale=w_scales[:],
+                    rhs=split_words[:].bitcast(FP4X4),
+                    rhs_scale=split_scales[:],
                     start=True,
                     stop=True,
                 )
@@ -211,7 +221,7 @@ def tile_retention_pa_t_kernel(
             singles, sums = products_of[r]
             own = term_pool.tile([P, TILES * 2 * DIM], F32, name="own")
             shared = term_pool.tile([P, TILES * DIM], F32, name="shared")
-            own_by = own[:].rearrange("p (w t d) -> p t w d", w=2, d=DIM)
+            own_by = own[:].rearrange("p (w t i o) -> p t w i o", w=2, i=PAIRS, o=2)
             def multiply_sums():
                 nc.vector.tensor_tensor(
                     out=shared[:].rearrange("p (w t i) -> p t w i", w=2, i=PAIRS),
@@ -226,10 +236,10 @@ def tile_retention_pa_t_kernel(
                 if r == 0 and bank == 1:
                     fill_factors(TILES)
                 nc.vector.tensor_tensor(
-                    out=own_by[:, 2 * bank : 2 * bank + 2, :, :],
-                    in0=singles[bank][:].rearrange("p (t w d) -> p t w d", w=2, d=DIM),
+                    out=own_by[:, 2 * bank : 2 * bank + 2, :, :, :],
+                    in0=singles[bank][:].rearrange("p (t o w i) -> p t w i o", o=2, w=2, i=PAIRS),
                     in1=factors[:, 2 * DIM * (first + 2 * bank) : 2 * DIM * (first + 2 * bank + 2)].rearrange(
-                        "p (t w d) -> p t w d", w=2, d=DIM
+                        "p (t w i o) -> p t w i o", w=2, i=PAIRS, o=2
                     ),
                     op=ALU.mult,
                 )
@@ -240,7 +250,7 @@ def tile_retention_pa_t_kernel(
         def subtract(engine, y, own, shared, n0, n1):
             engine.tensor_tensor(
                 out=y[:, 2 * n0 : 2 * n1].rearrange("p (n o) -> p n o", o=2),
-                in0=own[:].rearrange("p (n s) -> p n s", s=2)[:, n0:n1, ::-1],
+                in0=own[:].rearrange("p (n o) -> p n o", o=2)[:, n0:n1, :],
                 in1=shared[:, n0:n1].unsqueeze(2).to_broadcast([P, n1 - n0, 2]),
                 op=ALU.subtract,
             )
@@ -268,7 +278,7 @@ def tile_retention_pa_t_kernel(
                 n = slice(PAIRS * t0, PAIRS * t1)
                 nc.vector.tensor_tensor(
                     out=y[:].rearrange("p (w n o) -> p w n o", w=2, o=2),
-                    in0=own[:].rearrange("p (w n s) -> p w n s", w=2, s=2)[:, :, n, ::-1],
+                    in0=own[:].rearrange("p (w n o) -> p w n o", w=2, o=2)[:, :, n, :],
                     in1=shared[:]
                     .rearrange("p (w n) -> p w n", w=2)[:, :, n]
                     .unsqueeze(3)
@@ -285,12 +295,11 @@ def tile_retention_pa_t_kernel(
         sines = const.tile([P, 2, ROWS, PAIRS], F32)
         minus_cos = const.tile([P, ROWS, PAIRS], F32)
         factors = const.tile([P, ROWS * 2 * DIM], F32)
-        factors_by = factors[:].rearrange("p (j w i s) -> p w j i s", w=2, i=PAIRS, s=2)
+        factors_by = factors[:].rearrange("p (j w i o) -> p w j i o", w=2, i=PAIRS, o=2)
 
         def sine_and_cosine(first):
             js = slice(first, first + TILES)
-            nc.scalar.activation(out=size[:, js, :], in_=part[:, js, :], func=ACT.Abs)
-            for n, sign in enumerate((-1.0, 1.0)):
+            for n, sign in enumerate((1.0, -1.0)):
                 nc.scalar.activation(
                     out=sines[:, n, js, :], in_=part[:, js, :], func=ACT.Sin, scale=sign * TWO_PI
                 )
@@ -303,25 +312,18 @@ def tile_retention_pa_t_kernel(
             nc.vector.tensor_tensor(
                 out=factors_by[:, 0, js, :, :],
                 in0=minus_cos[:, js, :].unsqueeze(3).to_broadcast([P, TILES, PAIRS, 2]),
-                in1=sines[:, :, js, :].rearrange("p s j i -> p j i s"),
+                in1=sines[:, :, js, :].rearrange("p o j i -> p j i o"),
                 op=ALU.add,
             )
             if first == 0:
                 nc.vector.tensor_tensor(
                     out=factors_by[:, 1, js, :, :],
                     in0=minus_cos[:, js, :].unsqueeze(3).to_broadcast([P, TILES, PAIRS, 2]),
-                    in1=sines[:, :, js, :].rearrange("p s j i -> p j i s"),
+                    in1=sines[:, :, js, :].rearrange("p o j i -> p j i o"),
                     op=ALU.subtract,
                 )
             else:
-                nc.gpsimd.tensor_scalar(
-                    out=factors_by[:, 1, js, :, :],
-                    in0=factors_by[:, 0, js, :, ::-1],
-                    scalar1=1.0,
-                    scalar2=0.0,
-                    op0=ALU.mult,
-                    op1=ALU.add,
-                )
+                nc.scalar.copy(out=factors_by[:, 1, js, :, :], in_=factors_by[:, 0, js, :, ::-1])
 
         for o in range(2):
             nc.vector.tensor_copy(

@@ -22,7 +22,8 @@ PAIRS = DIM // 2
 ROWS = 8
 TILES = 4
 ROUNDS = HEADS * ROWS // TILES
-GPSIMD_PAIRS = 304
+GPSIMD_PAIRS = 320
+RELEASE_PAIRS = 384
 
 TWO_PI = 2.0 * math.pi
 ROPE_BASE = 10000.0
@@ -234,7 +235,8 @@ def tile_retention_pa_t_kernel(
                 multiply_sums()
             for bank in range(TILES // 2):
                 if r == 0 and bank == 1:
-                    fill_factors(TILES)
+                    fill_factors_of_q(TILES)
+                    fill_factors_of_k(TILES)
                 nc.vector.tensor_tensor(
                     out=own_by[:, 2 * bank : 2 * bank + 2, :, :, :],
                     in0=singles[bank][:].rearrange("p (t o w i) -> p t w i o", o=2, w=2, i=PAIRS),
@@ -265,7 +267,8 @@ def tile_retention_pa_t_kernel(
         def add_and_store(r):
             own, shared = terms_of[r]
             y = y_pool.tile([P, 2 * TILES * DIM], F32, name="y")
-            subtract(nc.vector, y, own, shared, GPSIMD_PAIRS - 1, 2 * TILES * PAIRS)
+            subtract(nc.vector, y, own, shared, GPSIMD_PAIRS - 1, RELEASE_PAIRS)
+            subtract(nc.vector, y, own, shared, RELEASE_PAIRS, 2 * TILES * PAIRS)
             subtract(nc.gpsimd, y, own, shared, 0, GPSIMD_PAIRS)
             for w in range(2):
                 store(r, w, 0, TILES, y[:, TILES * DIM * w : TILES * DIM * (w + 1)])
@@ -307,7 +310,7 @@ def tile_retention_pa_t_kernel(
                 out=minus_cos[:, js, :], in_=size[:, js, :], func=ACT.Sin, scale=TWO_PI, bias=-0.5 * math.pi
             )
 
-        def fill_factors(first):
+        def fill_factors_of_q(first):
             js = slice(first, first + TILES)
             nc.vector.tensor_tensor(
                 out=factors_by[:, 0, js, :, :],
@@ -315,15 +318,10 @@ def tile_retention_pa_t_kernel(
                 in1=sines[:, :, js, :].rearrange("p o j i -> p j i o"),
                 op=ALU.add,
             )
-            if first == 0:
-                nc.vector.tensor_tensor(
-                    out=factors_by[:, 1, js, :, :],
-                    in0=minus_cos[:, js, :].unsqueeze(3).to_broadcast([P, TILES, PAIRS, 2]),
-                    in1=sines[:, :, js, :].rearrange("p o j i -> p j i o"),
-                    op=ALU.subtract,
-                )
-            else:
-                nc.scalar.copy(out=factors_by[:, 1, js, :, :], in_=factors_by[:, 0, js, :, ::-1])
+
+        def fill_factors_of_k(first):
+            js = slice(first, first + TILES)
+            nc.scalar.copy(out=factors_by[:, 1, js, :, :], in_=factors_by[:, 0, js, :, ::-1])
 
         for o in range(2):
             nc.vector.tensor_copy(
@@ -332,8 +330,9 @@ def tile_retention_pa_t_kernel(
             )
         keep_warm(5)
         sine_and_cosine(0)
-        fill_factors(0)
+        fill_factors_of_q(0)
         transpose_and_regroup(0)
+        fill_factors_of_k(0)
         keep_warm(2)
         transpose_and_regroup(1)
         sine_and_cosine(TILES)

@@ -21,6 +21,7 @@ DIM = 128
 PAIRS = DIM // 2
 ROWS = 8
 TILES = 4
+SPLIT_TILES = 2
 ROUNDS = HEADS * ROWS // TILES
 GPSIMD_PAIRS = 320
 RELEASE_PAIRS = 384
@@ -45,6 +46,7 @@ def tile_retention_pa_t_kernel(
         x_pool = ctx.enter_context(tc.tile_pool(name="x", bufs=ROUNDS))
         grouped_pool = ctx.enter_context(tc.tile_pool(name="grouped", bufs=4))
         mx_pool = ctx.enter_context(tc.tile_pool(name="mx", bufs=3))
+        split_pool = ctx.enter_context(tc.tile_pool(name="split", bufs=4))
         term_pool = ctx.enter_context(tc.tile_pool(name="term", bufs=3))
         y_pool = ctx.enter_context(tc.tile_pool(name="y", bufs=5))
         xt_pool = ctx.enter_context(tc.psum_pool(name="xt", bufs=2))
@@ -157,6 +159,17 @@ def tile_retention_pa_t_kernel(
         grouped_of = {}
         products_of = {}
 
+        split_of = {}
+
+        def split(r):
+            x_split = split_pool.tile([P, SPLIT_TILES * K], BF16, name="x_split", align_bytes=64)
+            words = x_split[:].bitcast(F32).rearrange("p (t u w) -> p t u w", t=SPLIT_TILES, u=2)
+            nc.scalar.copy(
+                out=words,
+                in_=x_tiles[r][:, 0:SPLIT_TILES, :].bitcast(F32).rearrange("p t (w u) -> p t u w", u=2),
+            )
+            split_of[r] = words
+
         def transpose_and_regroup(r):
             x_words = x_tiles[r][:].bitcast(F32)
             grouped = grouped_pool.tile([P, TILES * K], BF16, name="grouped", align_bytes=64)
@@ -165,11 +178,11 @@ def tile_retention_pa_t_kernel(
                 xt = xt_pool.tile([P, 2, 2, P], F32, name="xt")
                 for t in range(2):
                     for u in range(2):
-                        nc.tensor.transpose(
-                            out=xt[:, t, u, :],
-                            in_=x_words[:, 2 * bank + t, u : K // 2 : 2],
-                            identity=ident[:],
-                        )
+                        if r in split_of and 2 * bank + t < SPLIT_TILES:
+                            words = split_of[r][:, 2 * bank + t, u, :]
+                        else:
+                            words = x_words[:, 2 * bank + t, u : K // 2 : 2]
+                        nc.tensor.transpose(out=xt[:, t, u, :], in_=words, identity=ident[:])
                 nc.scalar.copy(
                     out=grouped_words[:, 2 * bank : 2 * bank + 2, :, :],
                     in_=xt[:].rearrange("p t u r -> p t r u"),
@@ -217,7 +230,7 @@ def tile_retention_pa_t_kernel(
 
         terms_of = {}
 
-        def multiply(r):
+        def multiply(r, between=None):
             first = TILES * (r % 2)
             singles, sums = products_of[r]
             own = term_pool.tile([P, TILES * 2 * DIM], F32, name="own")
@@ -231,12 +244,11 @@ def tile_retention_pa_t_kernel(
                     op=ALU.mult,
                 )
 
-            if r == ROUNDS - 1:
+            if r >= ROUNDS - 2:
                 multiply_sums()
             for bank in range(TILES // 2):
-                if r == 0 and bank == 1:
-                    fill_factors_of_q(TILES)
-                    fill_factors_of_k(TILES)
+                if bank == 1 and between is not None:
+                    between()
                 nc.vector.tensor_tensor(
                     out=own_by[:, 2 * bank : 2 * bank + 2, :, :, :],
                     in0=singles[bank][:].rearrange("p (t o w i) -> p t w i o", o=2, w=2, i=PAIRS),
@@ -245,7 +257,7 @@ def tile_retention_pa_t_kernel(
                     ),
                     op=ALU.mult,
                 )
-            if r < ROUNDS - 1:
+            if r < ROUNDS - 2:
                 multiply_sums()
             terms_of[r] = (own, shared)
 
@@ -334,21 +346,28 @@ def tile_retention_pa_t_kernel(
         transpose_and_regroup(0)
         fill_factors_of_k(0)
         keep_warm(2)
-        transpose_and_regroup(1)
         sine_and_cosine(TILES)
+        transpose_and_regroup(1)
         keep_warm(1)
         quantise(0)
         for o in range(2):
             nc.vector.tensor_copy(out=split_scales[:, DIM * o : DIM * (o + 1)], in_=w_scales_by[:, 1 - o, :])
         multiply_by_weights(0)
+        fill_factors_of_q(TILES)
+        fill_factors_of_k(TILES)
 
         for r in range(ROUNDS):
             if r + 2 < ROUNDS:
                 transpose_and_regroup(r + 2)
+            if 2 <= r < ROUNDS - 4:
+                split(r + 4)
+            if r == 0:
+                multiply(r, between=lambda: quantise(1))
+                multiply_by_weights(1)
+                continue
             if r + 1 < ROUNDS:
                 quantise(r + 1)
                 multiply_by_weights(r + 1)
-            if r > 0:
-                add_and_store(r - 1)
+            add_and_store(r - 1)
             multiply(r)
         add_and_store_last(ROUNDS - 1)

import math
from contextlib import ExitStack

import concourse.mybir as mybir
from concourse.masks import make_identity

F32 = mybir.dt.float32
BF16 = mybir.dt.bfloat16
I32 = mybir.dt.int32
U32 = mybir.dt.uint32
U8 = mybir.dt.uint8
FP8X4 = mybir.dt.float8_e4m3fn_x4
FP4X4 = mybir.dt.float4_e2m1fn_x4
ALU = mybir.AluOpType
ACT = mybir.ActivationFunctionType

P = 128
HEADS = 8
K = 512
DIM = 128
PAIRS = DIM // 2
ROWS = 8
TILES = 4
SPLIT_TILES = 2
ROUNDS = HEADS * ROWS // TILES
GPSIMD_PAIRS = 320
RELEASE_PAIRS = 384

TWO_PI = 2.0 * math.pi
ROPE_BASE = 10000.0
ROUND_MAGIC = 12582912.0

FLOPS = 2 * HEADS * 1024 * K * 2 * DIM


def tile_retention_pa_t_kernel(
    tc, X, W_Q_words, W_Q_scales, W_K_words, W_K_scales, out_0, out_1
):
    nc = tc.nc
    x_rows = X.rearrange("b h (p j) k -> (b h) p j k", j=ROWS)
    out_rows = [o.rearrange("b h (p j) d -> (b h) p j d", j=ROWS) for o in (out_0, out_1)]

    with ExitStack() as ctx:
        ctx.enter_context(tc.manual_schedule())
        const = ctx.enter_context(tc.tile_pool(name="const", bufs=1))
        x_pool = ctx.enter_context(tc.tile_pool(name="x", bufs=ROUNDS))
        grouped_pool = ctx.enter_context(tc.tile_pool(name="grouped", bufs=4))
        mx_pool = ctx.enter_context(tc.tile_pool(name="mx", bufs=3))
        split_pool = ctx.enter_context(tc.tile_pool(name="split", bufs=4))
        term_pool = ctx.enter_context(tc.tile_pool(name="term", bufs=3))
        y_pool = ctx.enter_context(tc.tile_pool(name="y", bufs=5))
        xt_pool = ctx.enter_context(tc.psum_pool(name="xt", bufs=2))
        product_pool = ctx.enter_context(tc.psum_pool(name="product", bufs=6))

        x_tiles = []

        def load_x(r, t0=0, t1=TILES):
            if t0 == 0:
                x_tiles.append(x_pool.tile([P, TILES, K], BF16, name="x_sb"))
            first = TILES * (r % 2)
            nc.sync.dma_start(
                out=x_tiles[r][:, t0:t1, :], in_=x_rows[r // 2, :, first + t0 : first + t1, :]
            )

        w_words = const.tile([P, 2 * 2 * DIM], U8, align_bytes=64)
        w_scales = const.tile([P, 2 * DIM], U8, align_bytes=64)
        nc.vector.memset(w_scales[:].bitcast(I32), 0)

        def load_words(w, words):
            nc.sync.dma_start(
                out=w_words[:, 2 * DIM * w : 2 * DIM * (w + 1)].bitcast(I32), in_=words[0].bitcast(I32)
            )

        def load_scales(w, scales, quadrants):
            for quadrant in quadrants:
                nc.sync.dma_start(
                    out=w_scales[32 * quadrant : 32 * quadrant + 4, DIM * w : DIM * (w + 1)].bitcast(I32),
                    in_=scales[0, 4 * quadrant : 4 * quadrant + 4, :].bitcast(I32),
                )

        load_x(0, 0, TILES // 2)
        load_words(0, W_Q_words)
        load_words(1, W_K_words)
        load_x(0, TILES // 2, TILES)
        load_scales(0, W_Q_scales, range(3))
        load_x(1)
        load_scales(0, W_Q_scales, range(3, 4))
        load_scales(1, W_K_scales, range(4))
        for r in range(2, ROUNDS):
            load_x(r)

        warm = const.tile([P, 2], F32)
        nc.vector.memset(warm[:], 0.0)
        nc.scalar.activation(out=warm[:, 1:2], in_=warm[:, 0:1], func=ACT.Sin)

        zeros = const.tile([P, 4 * P], BF16)

        def keep_warm(count):
            idle = product_pool.tile([P, 4 * P], F32, name="product")
            for n in range(count):
                nc.tensor.matmul(out=idle[:], lhsT=zeros[:, 0:P], rhs=zeros[:], start=True, stop=True)

        position = const.tile([P, ROWS], F32)
        nc.gpsimd.iota(
            position[:],
            pattern=[[1, ROWS]],
            base=0,
            channel_multiplier=ROWS,
            allow_small_or_imprecise_dtypes=True,
        )
        nc.gpsimd.memset(zeros[:], 0.0)
        ident = const.tile([P, P], F32)
        make_identity(nc, ident[:])
        turns = const.tile([P, ROWS, PAIRS], F32)
        for i in range(4):
            nc.vector.tensor_scalar(
                out=turns[:, :, i : i + 1],
                in0=position[:].unsqueeze(2),
                scalar1=ROPE_BASE ** (-i / (PAIRS - 1)) / TWO_PI,
                scalar2=None,
                op0=ALU.mult,
            )
        for n in (4, 16):
            for part_of_four in range(1, 4):
                nc.vector.tensor_scalar(
                    out=turns[:, :, n * part_of_four : n * (part_of_four + 1)],
                    in0=turns[:, :, 0:n],
                    scalar1=ROPE_BASE ** (-n * part_of_four / (PAIRS - 1)),
                    scalar2=None,
                    op0=ALU.mult,
                )
        shifted = const.tile([P, ROWS, PAIRS], F32)
        nc.vector.tensor_scalar(
            out=shifted[:], in0=turns[:], scalar1=ROUND_MAGIC, scalar2=None, op0=ALU.add
        )
        part = const.tile([P, ROWS, PAIRS], F32)
        size = const.tile([P, ROWS, PAIRS], F32)
        for first in range(0, ROWS, TILES):
            js = slice(first, first + TILES)
            nc.vector.scalar_tensor_tensor(
                out=part[:, js, :],
                in0=shifted[:, js, :],
                scalar=ROUND_MAGIC,
                in1=turns[:, js, :],
                op0=ALU.subtract,
                op1=ALU.subtract,
            )
        for first in range(0, ROWS, TILES):
            js = slice(first, first + TILES)
            nc.vector.scalar_tensor_tensor(
                out=size[:, js, :],
                in0=part[:, js, :],
                scalar=-1.0,
                in1=part[:, js, :],
                op0=ALU.mult,
                op1=ALU.max,
            )

        grouped_of = {}
        products_of = {}

        split_of = {}

        def split(r):
            x_split = split_pool.tile([P, SPLIT_TILES * K], BF16, name="x_split", align_bytes=64)
            words = x_split[:].bitcast(F32).rearrange("p (t u w) -> p t u w", t=SPLIT_TILES, u=2)
            nc.scalar.copy(
                out=words,
                in_=x_tiles[r][:, 0:SPLIT_TILES, :].bitcast(F32).rearrange("p t (w u) -> p t u w", u=2),
            )
            split_of[r] = words

        def transpose_and_regroup(r):
            x_words = x_tiles[r][:].bitcast(F32)
            grouped = grouped_pool.tile([P, TILES * K], BF16, name="grouped", align_bytes=64)
            grouped_words = grouped[:].bitcast(F32).rearrange("p (t r u) -> p t r u", t=TILES, u=2)
            for bank in range(TILES // 2):
                xt = xt_pool.tile([P, 2, 2, P], F32, name="xt")
                for t in range(2):
                    for u in range(2):
                        if r in split_of and 2 * bank + t < SPLIT_TILES:
                            words = split_of[r][:, 2 * bank + t, u, :]
                        else:
                            words = x_words[:, 2 * bank + t, u : K // 2 : 2]
                        nc.tensor.transpose(out=xt[:, t, u, :], in_=words, identity=ident[:])
                nc.scalar.copy(
                    out=grouped_words[:, 2 * bank : 2 * bank + 2, :, :],
                    in_=xt[:].rearrange("p t u r -> p t r u"),
                )
            grouped_of[r] = grouped

        quantised_of = {}

        def quantise(r):
            codes = mx_pool.tile([P, TILES * P], U32, name="codes", align_bytes=64)
            scales = mx_pool.tile([P, TILES * P], U8, name="scales", align_bytes=64)
            nc.vector.quantize_mx(
                out=codes[:].bitcast(FP8X4), scales=scales[:], in_=grouped_of[r][:]
            )
            quantised_of[r] = (codes, scales)

        def multiply_by_weights(r):
            codes, scales = quantised_of[r]
            singles = [product_pool.tile([P, 2 * 2 * DIM], F32, name="product") for bank in range(TILES // 2)]
            sums = product_pool.tile([P, TILES * DIM], F32, name="product")
            for t in range(TILES):
                rows = slice(t * P, (t + 1) * P)
                nc.tensor.matmul_mx(
                    out=singles[t // 2][:, 2 * DIM * (t % 2) : 2 * DIM * (t % 2 + 1)],
                    lhsT=codes[:, rows].bitcast(FP8X4),
                    lhsT_scale=scales[:, rows],
                    rhs=split_words[:].bitcast(FP4X4),
                    rhs_scale=split_scales[:],
                    start=True,
                    stop=True,
                )
            for t in range(TILES):
                rows = slice(t * P, (t + 1) * P)
                for o in range(2):
                    nc.tensor.matmul_mx(
                        out=sums[:, DIM * t : DIM * (t + 1)],
                        lhsT=codes[:, rows].bitcast(FP8X4),
                        lhsT_scale=scales[:, rows],
                        rhs=split_words[:, 2 * DIM * o : 2 * DIM * (o + 1)].bitcast(FP4X4),
                        rhs_scale=split_scales[:, DIM * o : DIM * (o + 1)],
                        start=(o == 0),
                        stop=(o == 1),
                    )
            products_of[r] = (singles, sums)

        terms_of = {}

        def multiply(r, between=None):
            first = TILES * (r % 2)
            singles, sums = products_of[r]
            own = term_pool.tile([P, TILES * 2 * DIM], F32, name="own")
            shared = term_pool.tile([P, TILES * DIM], F32, name="shared")
            own_by = own[:].rearrange("p (w t i o) -> p t w i o", w=2, i=PAIRS, o=2)
            def multiply_sums():
                nc.vector.tensor_tensor(
                    out=shared[:].rearrange("p (w t i) -> p t w i", w=2, i=PAIRS),
                    in0=sums[:].rearrange("p (t w i) -> p t w i", w=2, i=PAIRS),
                    in1=minus_cos[:, first : first + TILES, :].unsqueeze(2).to_broadcast([P, TILES, 2, PAIRS]),
                    op=ALU.mult,
                )

            if r >= ROUNDS - 2:
                multiply_sums()
            for bank in range(TILES // 2):
                if bank == 1 and between is not None:
                    between()
                nc.vector.tensor_tensor(
                    out=own_by[:, 2 * bank : 2 * bank + 2, :, :, :],
                    in0=singles[bank][:].rearrange("p (t o w i) -> p t w i o", o=2, w=2, i=PAIRS),
                    in1=factors[:, 2 * DIM * (first + 2 * bank) : 2 * DIM * (first + 2 * bank + 2)].rearrange(
                        "p (t w i o) -> p t w i o", w=2, i=PAIRS, o=2
                    ),
                    op=ALU.mult,
                )
            if r < ROUNDS - 2:
                multiply_sums()
            terms_of[r] = (own, shared)

        def subtract(engine, y, own, shared, n0, n1):
            engine.tensor_tensor(
                out=y[:, 2 * n0 : 2 * n1].rearrange("p (n o) -> p n o", o=2),
                in0=own[:].rearrange("p (n o) -> p n o", o=2)[:, n0:n1, :],
                in1=shared[:, n0:n1].unsqueeze(2).to_broadcast([P, n1 - n0, 2]),
                op=ALU.subtract,
            )

        def store(r, w, t0, t1, y_rows):
            first = TILES * (r % 2)
            nc.sync.dma_start(
                out=out_rows[w][r // 2, :, first + t0 : first + t1, :],
                in_=y_rows.rearrange("p (j d) -> p j d", d=DIM),
            )

        def add_and_store(r):
            own, shared = terms_of[r]
            y = y_pool.tile([P, 2 * TILES * DIM], F32, name="y")
            subtract(nc.vector, y, own, shared, GPSIMD_PAIRS - 1, RELEASE_PAIRS)
            subtract(nc.vector, y, own, shared, RELEASE_PAIRS, 2 * TILES * PAIRS)
            subtract(nc.gpsimd, y, own, shared, 0, GPSIMD_PAIRS)
            for w in range(2):
                store(r, w, 0, TILES, y[:, TILES * DIM * w : TILES * DIM * (w + 1)])

        def add_and_store_last(r):
            own, shared = terms_of[r]
            for t0, t1 in ((0, 2), (2, 3), (3, 4)):
                width = DIM * (t1 - t0)
                y = y_pool.tile([P, 2 * width], F32, name="y")
                n = slice(PAIRS * t0, PAIRS * t1)
                nc.vector.tensor_tensor(
                    out=y[:].rearrange("p (w n o) -> p w n o", w=2, o=2),
                    in0=own[:].rearrange("p (w n o) -> p w n o", w=2, o=2)[:, :, n, :],
                    in1=shared[:]
                    .rearrange("p (w n) -> p w n", w=2)[:, :, n]
                    .unsqueeze(3)
                    .to_broadcast([P, 2, PAIRS * (t1 - t0), 2]),
                    op=ALU.subtract,
                )
                for w in range(2):
                    store(r, w, t0, t1, y[:, width * w : width * (w + 1)])

        split_words = const.tile([P, 2 * 2 * DIM], U8, align_bytes=64)
        split_scales = const.tile([P, 2 * DIM], U8, align_bytes=64)
        w_words_by = w_words[:].rearrange("p (n s b) -> p s n b", s=2, b=2)
        w_scales_by = w_scales[:].rearrange("p (n s) -> p s n", s=2)
        sines = const.tile([P, 2, ROWS, PAIRS], F32)
        minus_cos = const.tile([P, ROWS, PAIRS], F32)
        factors = const.tile([P, ROWS * 2 * DIM], F32)
        factors_by = factors[:].rearrange("p (j w i o) -> p w j i o", w=2, i=PAIRS, o=2)

        def sine_and_cosine(first):
            js = slice(first, first + TILES)
            for n, sign in enumerate((1.0, -1.0)):
                nc.scalar.activation(
                    out=sines[:, n, js, :], in_=part[:, js, :], func=ACT.Sin, scale=sign * TWO_PI
                )
            nc.scalar.activation(
                out=minus_cos[:, js, :], in_=size[:, js, :], func=ACT.Sin, scale=TWO_PI, bias=-0.5 * math.pi
            )

        def fill_factors_of_q(first):
            js = slice(first, first + TILES)
            nc.vector.tensor_tensor(
                out=factors_by[:, 0, js, :, :],
                in0=minus_cos[:, js, :].unsqueeze(3).to_broadcast([P, TILES, PAIRS, 2]),
                in1=sines[:, :, js, :].rearrange("p o j i -> p j i o"),
                op=ALU.add,
            )

        def fill_factors_of_k(first):
            js = slice(first, first + TILES)
            nc.scalar.copy(out=factors_by[:, 1, js, :, :], in_=factors_by[:, 0, js, :, ::-1])

        for o in range(2):
            nc.vector.tensor_copy(
                out=split_words[:, 2 * DIM * o : 2 * DIM * (o + 1)].rearrange("p (n b) -> p n b", b=2),
                in_=w_words_by[:, 1 - o, :, :],
            )
        keep_warm(5)
        sine_and_cosine(0)
        fill_factors_of_q(0)
        transpose_and_regroup(0)
        fill_factors_of_k(0)
        keep_warm(2)
        sine_and_cosine(TILES)
        transpose_and_regroup(1)
        keep_warm(1)
        quantise(0)
        for o in range(2):
            nc.vector.tensor_copy(out=split_scales[:, DIM * o : DIM * (o + 1)], in_=w_scales_by[:, 1 - o, :])
        multiply_by_weights(0)
        fill_factors_of_q(TILES)
        fill_factors_of_k(TILES)

        for r in range(ROUNDS):
            if r + 2 < ROUNDS:
                transpose_and_regroup(r + 2)
            if 2 <= r < ROUNDS - 4:
                split(r + 4)
            if r == 0:
                multiply(r, between=lambda: quantise(1))
                multiply_by_weights(1)
                continue
            if r + 1 < ROUNDS:
                quantise(r + 1)
                multiply_by_weights(r + 1)
            add_and_store(r - 1)
            multiply(r)
        add_and_store_last(ROUNDS - 1)
